import numpy as np
import ml_dtypes


def mxq(x, axis, fmt="e4m3"):
    dtype, down = {"e4m3": (ml_dtypes.float8_e4m3fn, 7), "e5m2": (ml_dtypes.float8_e5m2, 14)}[fmt]
    v = np.moveaxis(np.asarray(x, np.float32).astype(ml_dtypes.bfloat16).astype(np.float64), axis, -1)
    blocks = v.reshape(v.shape[:-1] + (-1, 32))
    amax = np.abs(blocks).max(-1, keepdims=True)
    byte = np.maximum(np.where(amax > 0, np.frexp(amax)[1] - 1 + 127, 0) - down, 1)
    scale = np.exp2(byte - 127.0)
    codes = (blocks / scale).astype(np.float32).astype(dtype).astype(np.float64)
    return np.moveaxis((codes * scale).reshape(v.shape), -1, axis)


WIDE = False


def mx_kscale(k):
    if not WIDE:
        return np.ones(k)
    levels = np.array([30, -30])
    if k % 512:
        return np.exp2(np.random.permutation(np.resize(levels, k // 32))).repeat(32)
    a = np.empty((k // 512, 16))
    for p in range(k // 512):
        a[p, :8] = np.random.permutation(np.resize(levels, 8))
        for g in range(8):
            far = levels[np.abs(levels - a[p, g]) >= 10]
            a[p, g + 8] = far[np.random.randint(len(far))]
    return np.exp2(a.ravel()).repeat(32)


BF16 = ml_dtypes.bfloat16


def bf(x):
    return np.asarray(x, np.float32).astype(BF16)


def f64(x):
    return np.asarray(x).astype(np.float64)


B, S, E, P, H = 2, 512, 1024, 1024, 8
D = P // H


def rope(x):
    inv_freq = 1.0 / (10000.0 ** (f64(np.arange(0, D, 2)) / D))
    t = f64(np.arange(S))
    freqs = np.repeat(t[:, None] * inv_freq[None, :], 2, axis=-1)
    cos, sin = np.cos(freqs), np.sin(freqs)
    xp = x.reshape(*x.shape[:-1], D // 2, 2)
    rot = np.stack((-xp[..., 1], xp[..., 0]), axis=-1).reshape(x.shape)
    return x * cos + rot * sin


def setup_inputs():
    s = mx_kscale(E)
    return {"emb": bf(np.random.standard_normal((B, S, E)) * s),
            "W1": bf(np.random.standard_normal((P, E)) * 0.6 / np.sqrt(E) / s),
            "W2": bf(np.random.standard_normal((P, E)) * 0.6 / np.sqrt(E) / s),
            "W3": bf(np.random.standard_normal((P, E)) * 2.0 / np.sqrt(E) / s)}


def reference(emb, W1, W2, W3):
    xq = mxq(f64(emb), 2, "e5m2")
    q = (xq @ mxq(f64(W1), 1, "e5m2").T).reshape(B, H, S, D)
    k = (xq @ mxq(f64(W2), 1, "e5m2").T).reshape(B, H, S, D)
    v = (xq @ mxq(f64(W3), 1, "e5m2").T).reshape(B, H, S, D)
    return rope(q), rope(k), v

@@ -1,0 +1,278 @@
+from contextlib import ExitStack
+
+import concourse.mybir as mybir
+from concourse.masks import make_identity
+
+F32 = mybir.dt.float32
+BF16 = mybir.dt.bfloat16
+I32 = mybir.dt.int32
+U32 = mybir.dt.uint32
+U8 = mybir.dt.uint8
+E5X4 = mybir.dt.float8_e5m2_x4
+ALU = mybir.AluOpType
+ACT = mybir.ActivationFunctionType
+
+PI = 3.141592653589793
+P = 128
+K = 1024
+FLOPS = 2 * 1024 * 1024 * 3072
+
+
+def tile_attention_pa_kernel(tc, emb, W1, W2, W3, out_0, out_1, out_2):
+    nc = tc.nc
+    emb_rows = emb.rearrange("b s e -> (b s) e")
+    weights = {"Q": W1, "K": W2, "V": W3}
+    outs = {
+        "Q": out_0.rearrange("b h (s c) d -> (b h s) (c d)", c=8),
+        "K": out_1.rearrange("b h (s c) d -> (b h s) (c d)", c=8),
+        "V": out_2.rearrange("b h (s c) d -> (b h s) (c d)", c=8),
+    }
+
+    with ExitStack() as ctx:
+        ctx.enter_context(tc.manual_schedule())
+        const = ctx.enter_context(tc.tile_pool(name="const", bufs=1))
+        grp = ctx.enter_context(tc.tile_pool(name="grp", bufs=2))
+        tpool = ctx.enter_context(tc.tile_pool(name="tpool", bufs=3))
+        ypool = ctx.enter_context(tc.tile_pool(name="ypool", bufs=3))
+        vpool = ctx.enter_context(tc.tile_pool(name="vpool", bufs=3))
+        psum = ctx.enter_context(tc.psum_pool(name="psum", bufs=8))
+
+        emb_words = {}
+        w_raw = {}
+
+        def load_emb(first, count):
+            raw = const.tile([P, count, K], BF16, name="raw_e%d" % first)
+            nc.sync.dma_start(
+                out=raw[:],
+                in_=emb_rows[first * P : (first + count) * P, :].rearrange("(m p) k -> p m k", p=P),
+            )
+            for i in range(count):
+                emb_words[first + i] = raw[:, i, :].bitcast(F32)
+
+        def load_weight(w, h, split):
+            raw = const.tile([P, 2, 2, K], BF16, name="raw_%s%d" % (w, h))
+            rows = weights[w][h * 512 : (h + 1) * 512, :]
+            if split:
+                for gi in range(2):
+                    nc.sync.dma_start(
+                        out=raw[:, gi, :, :].rearrange("p e k -> p (e k)"),
+                        in_=rows[gi * 256 : (gi + 1) * 256, :].rearrange("(p e) k -> p (e k)", e=2),
+                    )
+            else:
+                nc.sync.dma_start(
+                    out=raw[:].rearrange("p gi e k -> p gi (e k)"),
+                    in_=rows.rearrange("(gi p e) k -> p gi (e k)", gi=2, e=2),
+                )
+            w_raw[(w, h)] = raw
+
+        load_emb(0, 1)
+        load_weight("Q", 0, True)
+        load_emb(1, 1)
+        load_emb(2, 1)
+        load_emb(3, 1)
+        load_weight("Q", 1, False)
+        load_emb(4, 4)
+        load_weight("V", 0, False)
+        load_weight("V", 1, False)
+        load_weight("K", 0, False)
+        load_weight("K", 1, False)
+
+        zero = const.tile([P, 1], F32, name="zero")
+        warm = const.tile([P, 1], F32, name="warm")
+        nc.vector.memset(zero[:], 0.0)
+        nc.scalar.activation(out=warm[:], in_=zero[:], func=ACT.Sin)
+
+        pos_i = const.tile([P, 8], I32, name="pos_i")
+        nc.gpsimd.iota(pos_i[0:64, :], pattern=[[1, 8]], base=0, channel_multiplier=8)
+        nc.gpsimd.iota(pos_i[64:128, :], pattern=[[1, 8]], base=0, channel_multiplier=8)
+        ident = const.tile([P, P], F32, name="ident")
+        make_identity(nc, ident[:])
+
+        ratio = 10000.0 ** (-1.0 / 64.0)
+        gtab = const.tile([P, 64], F32, name="gtab")
+        nc.vector.memset(gtab[:, 0:1], 1.0)
+        for k in range(6):
+            n = 1 << k
+            nc.vector.tensor_scalar_mul(out=gtab[:, n : 2 * n], in0=gtab[:, 0:n], scalar1=ratio ** n)
+        pos_f = const.tile([P, 8], F32, name="pos_f")
+        nc.vector.tensor_copy(out=pos_f[:], in_=pos_i[:])
+        turns = const.tile([P, 8, 64], F32, name="turns")
+        nc.vector.scalar_tensor_tensor(
+            out=turns[:],
+            in0=pos_f[:].unsqueeze(2).to_broadcast([P, 8, 64]),
+            scalar=1.0 / (2.0 * PI),
+            in1=gtab[:].unsqueeze(1).to_broadcast([P, 8, 64]),
+            op0=ALU.mult,
+            op1=ALU.mult,
+        )
+        turns_flat = turns[:].rearrange("p c i -> p (c i)")
+        whole_i = const.tile([P, 512], I32, name="whole_i")
+        nc.vector.tensor_copy(out=whole_i[:], in_=turns_flat)
+        whole_f = const.tile([P, 512], F32, name="whole_f")
+        nc.vector.tensor_copy(out=whole_f[:], in_=whole_i[:])
+        frac = const.tile([P, 512], F32, name="frac")
+        nc.vector.tensor_tensor(out=frac[:], in0=turns_flat, in1=whole_f[:], op=ALU.subtract)
+        nfrac = const.tile([P, 512], F32, name="nfrac")
+        nc.vector.scalar_tensor_tensor(
+            out=nfrac[:], in0=frac[:], scalar=0.5, in1=frac[:], op0=ALU.is_ge, op1=ALU.subtract
+        )
+        table = const.tile([P, 2, 1024], F32, name="table")
+        table_v = table[:].rearrange("p r (bg e q) -> p r bg e q", bg=4, e=2, q=P)
+
+        def build_table():
+            absn = const.tile([P, 512], F32, name="absn")
+            nc.scalar.activation(out=absn[:], in_=nfrac[:], func=ACT.Abs)
+            absn_v = absn[:].rearrange("p (bg q) -> p bg q", bg=4)
+            nfrac_v = nfrac[:].rearrange("p (bg q) -> p bg q", bg=4)
+            two_pi = 2.0 * PI
+            nc.scalar.activation(out=table_v[:, 0, :, 0, :], in_=absn_v, func=ACT.Sin, scale=-two_pi, bias=0.5 * PI)
+            nc.scalar.activation(out=table_v[:, 0, :, 1, :], in_=nfrac_v, func=ACT.Sin, scale=two_pi)
+            nc.scalar.activation(out=table_v[:, 1, :, 0, :], in_=nfrac_v, func=ACT.Sin, scale=-two_pi)
+            nc.scalar.activation(out=table_v[:, 1, :, 1, :], in_=absn_v, func=ACT.Sin, scale=-two_pi, bias=0.5 * PI)
+
+        grouped_e = const.tile([P, 8, 2, P, 4], BF16, name="grouped_e", align_bytes=64)
+        grouped_e_flat = grouped_e[:].rearrange("p m g r j -> p (m g r j)")
+        codes_e = const.tile([P, 2048], U32, name="codes_e", align_bytes=64)
+        scales_e = const.tile([P, 2048], U8, name="scales_e", align_bytes=64)
+        codes_w = {}
+        scales_w = {}
+        grouped_w = {}
+
+        def transpose_block(words, dst, engine):
+            bank = psum.tile([P, 2, 2, P], F32, name="tp", tag="bank")
+            for g in range(2):
+                for u in range(2):
+                    nc.tensor.transpose(bank[:, g, u, :], words[:, 256 * g + u : 256 * (g + 1) : 2], ident[:])
+            src = bank[:].rearrange("p g u r -> p g r u")
+            if engine == "S":
+                nc.scalar.copy(out=dst, in_=src)
+            else:
+                nc.vector.tensor_copy(out=dst, in_=src)
+
+        def prep_emb(m, engine):
+            transpose_block(emb_words[m], grouped_e[:, m, :, :, :].bitcast(F32), engine)
+
+        def quant_emb(first, count):
+            lo = first * 256
+            hi = (first + count) * 256
+            nc.vector.quantize_mx(
+                out=codes_e[:, lo:hi].bitcast(E5X4), scales=scales_e[:, lo:hi], in_=grouped_e_flat[:, 4 * lo : 4 * hi]
+            )
+
+        def prep_weight(w, h, engine):
+            grouped = grp.tile([P, 2, 512, 4], BF16, name="grouped_w", tag="grouped_w", align_bytes=64)
+            grouped_w[(w, h)] = grouped
+            for gi in range(2):
+                for e in range(2):
+                    n0 = gi * 256 + e * P
+                    transpose_block(
+                        w_raw[(w, h)][:, gi, e, :].bitcast(F32), grouped[:].bitcast(F32)[:, :, n0 : n0 + P, :], engine
+                    )
+
+        def quant_weight(w, h, pieces):
+            codes = const.tile([P, 1024], U32, name="codes_%s%d" % (w, h), align_bytes=64)
+            scales = const.tile([P, 1024], U8, name="scales_%s%d" % (w, h), align_bytes=64)
+            codes_w[(w, h)] = codes
+            scales_w[(w, h)] = scales
+            flat = grouped_w[(w, h)][:].rearrange("p g n j -> p (g n j)")
+            step = 1024 // pieces
+            for i in range(pieces):
+                lo = i * step
+                hi = lo + step
+                nc.vector.quantize_mx(
+                    out=codes[:, lo:hi].bitcast(E5X4), scales=scales[:, lo:hi], in_=flat[:, 4 * lo : 4 * hi]
+                )
+
+        def project(w, m, h):
+            acc = psum.tile([P, 512], F32, name="acc", tag="bank")
+            for g in range(2):
+                lo = (2 * m + g) * P
+                nc.tensor.matmul_mx(
+                    out=acc[:],
+                    lhsT=codes_e[:, lo : lo + P].bitcast(E5X4),
+                    lhsT_scale=scales_e[:, lo : lo + P],
+                    rhs=codes_w[(w, h)][:, g * 512 : (g + 1) * 512].bitcast(E5X4),
+                    rhs_scale=scales_w[(w, h)][:, g * 512 : (g + 1) * 512],
+                    start=(g == 0),
+                    stop=(g == 1),
+                )
+            return acc
+
+        def rope_products(acc, h, prod, slot):
+            nc.vector.tensor_tensor(
+                out=prod[:, :, slot, :],
+                in0=acc[:].unsqueeze(1).to_broadcast([P, 2, 512]),
+                in1=table[:, :, h * 512 : (h + 1) * 512],
+                op=ALU.mult,
+            )
+
+        def rope_sum_store(prod, pair):
+            y = ypool.tile([P, 2, 512], F32, name="y", tag="y")
+            pv = prod[:].rearrange("p r b (gi e q) -> p (b gi) q r e", gi=2, e=2, q=P)
+            nc.gpsimd.tensor_tensor(
+                out=y[:].rearrange("p b (gi q r) -> p (b gi) q r", gi=2, q=P, r=2),
+                in0=pv[:, :, :, :, 0],
+                in1=pv[:, :, :, :, 1],
+                op=ALU.add,
+            )
+            (w, m0, h0), (w1, m1, h1) = pair
+            if m0 == m1:
+                nc.sync.dma_start(out=outs[w][m0 * P : (m0 + 1) * P, :], in_=y[:].rearrange("p b c -> p (b c)"))
+            else:
+                nc.sync.dma_start(
+                    out=outs[w][m0 * P : (m0 + 2) * P, h0 * 512 : (h0 + 1) * 512].rearrange("(b p) c -> p b c", b=2),
+                    in_=y[:],
+                )
+
+        prep_emb(0, "S")
+        build_table()
+        quant_emb(0, 1)
+        prep_weight("Q", 0, "V")
+        prep_emb(1, "S")
+        prep_emb(2, "S")
+        prep_emb(3, "S")
+        quant_weight("Q", 0, 2)
+        quant_emb(1, 1)
+
+        pairs = [
+            (("Q", 0, 0), ("Q", 1, 0)),
+            (("Q", 2, 0), ("Q", 3, 0)),
+            (("Q", 0, 1), ("Q", 1, 1)),
+            (("Q", 2, 1), ("Q", 3, 1)),
+        ]
+        pairs.extend([(("Q", m, 0), ("Q", m, 1)) for m in range(4, 8)])
+        pairs.extend([(("K", m, 0), ("K", m, 1)) for m in range(8)])
+        runs = [("Q", 1), ("E", 4), ("V", 0), ("V", 1), ("K", 0), ("K", 1)]
+
+        for j in range(16):
+            pair = pairs[j]
+            accs = [project(w, m, h) for (w, m, h) in pair]
+            vaccs = []
+            if j < 6:
+                if runs[j][0] == "E":
+                    for m in range(4, 8):
+                        prep_emb(m, "S")
+                else:
+                    prep_weight(runs[j][0], runs[j][1], "S")
+            elif j < 14:
+                vaccs = [project("V", j - 6, h) for h in range(2)]
+            prod = tpool.tile([P, 2, 2, 512], F32, name="prod", tag="prod")
+            rope_products(accs[0], pair[0][2], prod, 0)
+            if j == 0:
+                quant_emb(2, 2)
+            rope_products(accs[1], pair[1][2], prod, 1)
+            if 1 <= j <= 6:
+                if runs[j - 1][0] == "E":
+                    quant_emb(4, 4)
+                else:
+                    quant_weight(runs[j - 1][0], runs[j - 1][1], 1)
+            rope_sum_store(prod, pair)
+            if vaccs:
+                yv = vpool.tile([P, 2, 512], F32, name="yv", tag="yv")
+                for h in range(2):
+                    nc.scalar.copy(
+                        out=yv[:, h, :].rearrange("p (gi q e) -> p gi q e", gi=2, q=P, e=2),
+                        in_=vaccs[h][:].rearrange("p (gi e q) -> p gi q e", gi=2, e=2, q=P),
+                    )
+                mv = j - 6
+                nc.scalar.dma_start(out=outs["V"][mv * P : (mv + 1) * P, :], in_=yv[:].rearrange("p b c -> p (b c)"))

@@ -108,27 +108,34 @@ def tile_attention_pa_kernel(tc, emb, W1, W2, W3, out_0, out_1, out_2):
         turns_flat = turns[:].rearrange("p c i -> p (c i)")
         whole_i = const.tile([P, 512], I32, name="whole_i")
         nc.vector.tensor_copy(out=whole_i[:], in_=turns_flat)
-        whole_f = const.tile([P, 512], F32, name="whole_f")
-        nc.vector.tensor_copy(out=whole_f[:], in_=whole_i[:])
         frac = const.tile([P, 512], F32, name="frac")
-        nc.vector.tensor_tensor(out=frac[:], in0=turns_flat, in1=whole_f[:], op=ALU.subtract)
+        nc.vector.tensor_tensor(out=frac[:], in0=turns_flat, in1=whole_i[:], op=ALU.subtract)
         nfrac = const.tile([P, 512], F32, name="nfrac")
         nc.vector.scalar_tensor_tensor(
             out=nfrac[:], in0=frac[:], scalar=0.5, in1=frac[:], op0=ALU.is_ge, op1=ALU.subtract
         )
-        table = const.tile([P, 2, 1024], F32, name="table")
-        table_v = table[:].rearrange("p r (bg e q) -> p r bg e q", bg=4, e=2, q=P)
+        trig = const.tile([P, 3, 512], F32, name="trig")
+        table = const.tile([P, 2, 2, 256, 2], F32, name="table")
 
-        def build_table():
+        def build_trig():
             absn = const.tile([P, 512], F32, name="absn")
-            nc.scalar.activation(out=absn[:], in_=nfrac[:], func=ACT.Abs)
-            absn_v = absn[:].rearrange("p (bg q) -> p bg q", bg=4)
-            nfrac_v = nfrac[:].rearrange("p (bg q) -> p bg q", bg=4)
             two_pi = 2.0 * PI
-            nc.scalar.activation(out=table_v[:, 0, :, 0, :], in_=absn_v, func=ACT.Sin, scale=-two_pi, bias=0.5 * PI)
-            nc.scalar.activation(out=table_v[:, 0, :, 1, :], in_=nfrac_v, func=ACT.Sin, scale=two_pi)
-            nc.scalar.activation(out=table_v[:, 1, :, 0, :], in_=nfrac_v, func=ACT.Sin, scale=-two_pi)
-            nc.scalar.activation(out=table_v[:, 1, :, 1, :], in_=absn_v, func=ACT.Sin, scale=-two_pi, bias=0.5 * PI)
+            nc.scalar.activation(out=absn[:], in_=nfrac[:], func=ACT.Abs)
+            nc.scalar.activation(out=trig[:, 1, :], in_=absn[:], func=ACT.Sin, scale=-two_pi, bias=0.5 * PI)
+            nc.scalar.activation(out=trig[:, 2, :], in_=nfrac[:], func=ACT.Sin, scale=-two_pi)
+            nc.scalar.activation(out=trig[:, 0, :], in_=nfrac[:], func=ACT.Sin, scale=two_pi)
+
+        def build_table(h):
+            for e in range(2):
+                first = 1 - e
+                nc.gpsimd.tensor_scalar(
+                    out=table[:, h, e, :, :],
+                    in0=trig[:, first : first + 2, h * 256 : (h + 1) * 256].rearrange("p r x -> p x r"),
+                    scalar1=1.0,
+                    scalar2=0.0,
+                    op0=ALU.mult,
+                    op1=ALU.add,
+                )
 
         grouped_e = const.tile([P, 8, 2, P, 4], BF16, name="grouped_e", align_bytes=64)
         grouped_e_flat = grouped_e[:].rearrange("p m g r j -> p (m g r j)")
@@ -159,14 +166,16 @@ def tile_attention_pa_kernel(tc, emb, W1, W2, W3, out_0, out_1, out_2):
                 out=codes_e[:, lo:hi].bitcast(E5X4), scales=scales_e[:, lo:hi], in_=grouped_e_flat[:, 4 * lo : 4 * hi]
             )
 
-        def prep_weight(w, h, engine):
+        def prep_weight(w, h, engines):
             grouped = grp.tile([P, 2, 512, 4], BF16, name="grouped_w", tag="grouped_w", align_bytes=64)
             grouped_w[(w, h)] = grouped
             for gi in range(2):
                 for e in range(2):
-                    n0 = gi * 256 + e * P
+                    n0 = e * 256 + gi * P
                     transpose_block(
-                        w_raw[(w, h)][:, gi, e, :].bitcast(F32), grouped[:].bitcast(F32)[:, :, n0 : n0 + P, :], engine
+                        w_raw[(w, h)][:, gi, e, :].bitcast(F32),
+                        grouped[:].bitcast(F32)[:, :, n0 : n0 + P, :],
+                        engines[2 * gi + e],
                     )
 
         def quant_weight(w, h, pieces):
@@ -200,21 +209,13 @@ def tile_attention_pa_kernel(tc, emb, W1, W2, W3, out_0, out_1, out_2):
 
         def rope_products(acc, h, prod, slot):
             nc.vector.tensor_tensor(
-                out=prod[:, :, slot, :],
-                in0=acc[:].unsqueeze(1).to_broadcast([P, 2, 512]),
-                in1=table[:, :, h * 512 : (h + 1) * 512],
+                out=prod[:, slot, :, :].rearrange("p e (x r) -> p (e x) r", r=2),
+                in0=acc[:].unsqueeze(2).to_broadcast([P, 512, 2]),
+                in1=table[:, h, :, :, :].rearrange("p e x r -> p (e x) r"),
                 op=ALU.mult,
             )
 
-        def rope_sum_store(prod, pair):
-            y = ypool.tile([P, 2, 512], F32, name="y", tag="y")
-            pv = prod[:].rearrange("p r b (gi e q) -> p (b gi) q r e", gi=2, e=2, q=P)
-            nc.gpsimd.tensor_tensor(
-                out=y[:].rearrange("p b (gi q r) -> p (b gi) q r", gi=2, q=P, r=2),
-                in0=pv[:, :, :, :, 0],
-                in1=pv[:, :, :, :, 1],
-                op=ALU.add,
-            )
+        def store_pair(y, pair):
             (w, m0, h0), (w1, m1, h1) = pair
             if m0 == m1:
                 nc.sync.dma_start(out=outs[w][m0 * P : (m0 + 1) * P, :], in_=y[:].rearrange("p b c -> p (b c)"))
@@ -224,10 +225,17 @@ def tile_attention_pa_kernel(tc, emb, W1, W2, W3, out_0, out_1, out_2):
                     in_=y[:],
                 )
 
+        def rope_sum_store(prod, pair):
+            y = ypool.tile([P, 2, 512], F32, name="y", tag="y")
+            nc.gpsimd.tensor_tensor(out=y[:], in0=prod[:, :, 0, :], in1=prod[:, :, 1, :], op=ALU.add)
+            store_pair(y, pair)
+
         prep_emb(0, "S")
-        build_table()
+        build_trig()
+        build_table(0)
+        build_table(1)
         quant_emb(0, 1)
-        prep_weight("Q", 0, "V")
+        prep_weight("Q", 0, "VVVS")
         prep_emb(1, "S")
         prep_emb(2, "S")
         prep_emb(3, "S")
@@ -253,26 +261,36 @@ def tile_attention_pa_kernel(tc, emb, W1, W2, W3, out_0, out_1, out_2):
                     for m in range(4, 8):
                         prep_emb(m, "S")
                 else:
-                    prep_weight(runs[j][0], runs[j][1], "S")
+                    prep_weight(runs[j][0], runs[j][1], "SSSS")
             elif j < 14:
                 vaccs = [project("V", j - 6, h) for h in range(2)]
             prod = tpool.tile([P, 2, 2, 512], F32, name="prod", tag="prod")
-            rope_products(accs[0], pair[0][2], prod, 0)
-            if j == 0:
-                quant_emb(2, 2)
-            rope_products(accs[1], pair[1][2], prod, 1)
-            if 1 <= j <= 6:
-                if runs[j - 1][0] == "E":
-                    quant_emb(4, 4)
-                else:
-                    quant_weight(runs[j - 1][0], runs[j - 1][1], 1)
-            rope_sum_store(prod, pair)
+            if j == 15:
+                y = ypool.tile([P, 2, 512], F32, name="y", tag="y")
+                for slot in range(2):
+                    (w, m, h) = pair[slot]
+                    rope_products(accs[slot], h, prod, slot)
+                    nc.vector.tensor_tensor(
+                        out=y[:, slot, :], in0=prod[:, slot, 0, :], in1=prod[:, slot, 1, :], op=ALU.add
+                    )
+                    nc.sync.dma_start(out=outs[w][m * P : (m + 1) * P, h * 512 : (h + 1) * 512], in_=y[:, slot, :])
+            else:
+                rope_products(accs[0], pair[0][2], prod, 0)
+                if j == 0:
+                    quant_emb(2, 2)
+                rope_products(accs[1], pair[1][2], prod, 1)
+                if 1 <= j <= 6:
+                    if runs[j - 1][0] == "E":
+                        quant_emb(4, 4)
+                    else:
+                        quant_weight(runs[j - 1][0], runs[j - 1][1], 2 if j == 1 else 1)
+                rope_sum_store(prod, pair)
             if vaccs:
                 yv = vpool.tile([P, 2, 512], F32, name="yv", tag="yv")
                 for h in range(2):
                     nc.scalar.copy(
-                        out=yv[:, h, :].rearrange("p (gi q e) -> p gi q e", gi=2, q=P, e=2),
-                        in_=vaccs[h][:].rearrange("p (gi e q) -> p gi q e", gi=2, e=2, q=P),
+                        out=yv[:, h, :].rearrange("p (x e) -> p x e", e=2),
+                        in_=vaccs[h][:].rearrange("p (e x) -> p x e", e=2),
                     )
                 mv = j - 6
                 nc.scalar.dma_start(out=outs["V"][mv * P : (mv + 1) * P, :], in_=yv[:].rearrange("p b c -> p (b c)"))

@@ -16,6 +16,8 @@ PI = 3.141592653589793
 P = 128
 K = 1024
 FLOPS = 2 * 1024 * 1024 * 3072
+GCOLS = 416
+GCOLS_BY_STEP = {14: 208}
 
 
 def tile_attention_pa_kernel(tc, emb, W1, W2, W3, out_0, out_1, out_2):
@@ -31,8 +33,8 @@ def tile_attention_pa_kernel(tc, emb, W1, W2, W3, out_0, out_1, out_2):
     with ExitStack() as ctx:
         ctx.enter_context(tc.manual_schedule())
         const = ctx.enter_context(tc.tile_pool(name="const", bufs=1))
-        grp = ctx.enter_context(tc.tile_pool(name="grp", bufs=2))
-        tpool = ctx.enter_context(tc.tile_pool(name="tpool", bufs=3))
+        grp = ctx.enter_context(tc.tile_pool(name="grp", bufs=3))
+        tpool = ctx.enter_context(tc.tile_pool(name="tpool", bufs=4))
         ypool = ctx.enter_context(tc.tile_pool(name="ypool", bufs=3))
         vpool = ctx.enter_context(tc.tile_pool(name="vpool", bufs=3))
         psum = ctx.enter_context(tc.psum_pool(name="psum", bufs=8))
@@ -49,15 +51,17 @@ def tile_attention_pa_kernel(tc, emb, W1, W2, W3, out_0, out_1, out_2):
             for i in range(count):
                 emb_words[first + i] = raw[:, i, :].bitcast(F32)
 
-        def load_weight(w, h, split):
+        def block_order(w):
+            first_e = 0 if w == "V" else 1
+            return [(0, first_e), (1, first_e), (0, 1 - first_e), (1, 1 - first_e)]
+
+        def load_weight(w, h, by_block):
             raw = const.tile([P, 2, 2, K], BF16, name="raw_%s%d" % (w, h))
             rows = weights[w][h * 512 : (h + 1) * 512, :]
-            if split:
-                for gi in range(2):
-                    nc.sync.dma_start(
-                        out=raw[:, gi, :, :].rearrange("p e k -> p (e k)"),
-                        in_=rows[gi * 256 : (gi + 1) * 256, :].rearrange("(p e) k -> p (e k)", e=2),
-                    )
+            if by_block:
+                view = rows.rearrange("(gi p e) k -> p gi e k", gi=2, e=2)
+                for gi, e in block_order(w):
+                    nc.sync.dma_start(out=raw[:, gi, e, :], in_=view[:, gi, e, :])
             else:
                 nc.sync.dma_start(
                     out=raw[:].rearrange("p gi e k -> p gi (e k)"),
@@ -67,11 +71,9 @@ def tile_attention_pa_kernel(tc, emb, W1, W2, W3, out_0, out_1, out_2):
 
         load_emb(0, 1)
         load_weight("Q", 0, True)
-        load_emb(1, 1)
-        load_emb(2, 1)
-        load_emb(3, 1)
+        for m in range(1, 8):
+            load_emb(m, 1)
         load_weight("Q", 1, False)
-        load_emb(4, 4)
         load_weight("V", 0, False)
         load_weight("V", 1, False)
         load_weight("K", 0, False)
@@ -94,12 +96,10 @@ def tile_attention_pa_kernel(tc, emb, W1, W2, W3, out_0, out_1, out_2):
         for k in range(6):
             n = 1 << k
             nc.vector.tensor_scalar_mul(out=gtab[:, n : 2 * n], in0=gtab[:, 0:n], scalar1=ratio ** n)
-        pos_f = const.tile([P, 8], F32, name="pos_f")
-        nc.vector.tensor_copy(out=pos_f[:], in_=pos_i[:])
         turns = const.tile([P, 8, 64], F32, name="turns")
         nc.vector.scalar_tensor_tensor(
             out=turns[:],
-            in0=pos_f[:].unsqueeze(2).to_broadcast([P, 8, 64]),
+            in0=pos_i[:].unsqueeze(2).to_broadcast([P, 8, 64]),
             scalar=1.0 / (2.0 * PI),
             in1=gtab[:].unsqueeze(1).to_broadcast([P, 8, 64]),
             op0=ALU.mult,
@@ -114,28 +114,17 @@ def tile_attention_pa_kernel(tc, emb, W1, W2, W3, out_0, out_1, out_2):
         nc.vector.scalar_tensor_tensor(
             out=nfrac[:], in0=frac[:], scalar=0.5, in1=frac[:], op0=ALU.is_ge, op1=ALU.subtract
         )
-        trig = const.tile([P, 3, 512], F32, name="trig")
-        table = const.tile([P, 2, 2, 256, 2], F32, name="table")
+        absn = const.tile([P, 512], F32, name="absn")
+        trig = const.tile([P, 2, 2, 512], F32, name="trig")
 
-        def build_trig():
-            absn = const.tile([P, 512], F32, name="absn")
+        def build_trig(h):
+            cols = slice(h * 256, (h + 1) * 256)
             two_pi = 2.0 * PI
-            nc.scalar.activation(out=absn[:], in_=nfrac[:], func=ACT.Abs)
-            nc.scalar.activation(out=trig[:, 1, :], in_=absn[:], func=ACT.Sin, scale=-two_pi, bias=0.5 * PI)
-            nc.scalar.activation(out=trig[:, 2, :], in_=nfrac[:], func=ACT.Sin, scale=-two_pi)
-            nc.scalar.activation(out=trig[:, 0, :], in_=nfrac[:], func=ACT.Sin, scale=two_pi)
-
-        def build_table(h):
-            for e in range(2):
-                first = 1 - e
-                nc.gpsimd.tensor_scalar(
-                    out=table[:, h, e, :, :],
-                    in0=trig[:, first : first + 2, h * 256 : (h + 1) * 256].rearrange("p r x -> p x r"),
-                    scalar1=1.0,
-                    scalar2=0.0,
-                    op0=ALU.mult,
-                    op1=ALU.add,
-                )
+            nc.scalar.activation(out=absn[:, cols], in_=nfrac[:, cols], func=ACT.Abs)
+            nc.scalar.activation(out=trig[:, 0, 0, cols], in_=nfrac[:, cols], func=ACT.Sin, scale=two_pi)
+            nc.scalar.activation(out=trig[:, 0, 1, cols], in_=absn[:, cols], func=ACT.Sin, scale=-two_pi, bias=0.5 * PI)
+            nc.scalar.activation(out=trig[:, 1, 0, cols], in_=absn[:, cols], func=ACT.Sin, scale=-two_pi, bias=0.5 * PI)
+            nc.scalar.activation(out=trig[:, 1, 1, cols], in_=nfrac[:, cols], func=ACT.Sin, scale=-two_pi)
 
         grouped_e = const.tile([P, 8, 2, P, 4], BF16, name="grouped_e", align_bytes=64)
         grouped_e_flat = grouped_e[:].rearrange("p m g r j -> p (m g r j)")
@@ -145,19 +134,28 @@ def tile_attention_pa_kernel(tc, emb, W1, W2, W3, out_0, out_1, out_2):
         scales_w = {}
         grouped_w = {}
 
-        def transpose_block(words, dst, engine):
+        def transpose_block(words):
             bank = psum.tile([P, 2, 2, P], F32, name="tp", tag="bank")
             for g in range(2):
                 for u in range(2):
                     nc.tensor.transpose(bank[:, g, u, :], words[:, 256 * g + u : 256 * (g + 1) : 2], ident[:])
-            src = bank[:].rearrange("p g u r -> p g r u")
+            return bank
+
+        def copy_out(engine, dst, src):
             if engine == "S":
                 nc.scalar.copy(out=dst, in_=src)
             else:
                 nc.vector.tensor_copy(out=dst, in_=src)
 
-        def prep_emb(m, engine):
-            transpose_block(emb_words[m], grouped_e[:, m, :, :, :].bitcast(F32), engine)
+        def evacuate(bank, dst, engines):
+            if len(engines) == 1:
+                copy_out(engines, dst, bank[:].rearrange("p g u r -> p g r u"))
+            else:
+                for g in range(2):
+                    copy_out(engines[g], dst[:, g, :, :], bank[:, g, :, :].rearrange("p u r -> p r u"))
+
+        def prep_emb(m, engines):
+            evacuate(transpose_block(emb_words[m]), grouped_e[:, m, :, :, :].bitcast(F32), engines)
 
         def quant_emb(first, count):
             lo = first * 256
@@ -166,31 +164,26 @@ def tile_attention_pa_kernel(tc, emb, W1, W2, W3, out_0, out_1, out_2):
                 out=codes_e[:, lo:hi].bitcast(E5X4), scales=scales_e[:, lo:hi], in_=grouped_e_flat[:, 4 * lo : 4 * hi]
             )
 
-        def prep_weight(w, h, engines):
-            grouped = grp.tile([P, 2, 512, 4], BF16, name="grouped_w", tag="grouped_w", align_bytes=64)
-            grouped_w[(w, h)] = grouped
-            for gi in range(2):
-                for e in range(2):
-                    n0 = e * 256 + gi * P
-                    transpose_block(
-                        w_raw[(w, h)][:, gi, e, :].bitcast(F32),
-                        grouped[:].bitcast(F32)[:, :, n0 : n0 + P, :],
-                        engines[2 * gi + e],
-                    )
+        def open_weight(w, h):
+            grouped_w[(w, h)] = grp.tile([P, 2, 512, 4], BF16, name="grouped_w", tag="grouped_w", align_bytes=64)
+            codes_w[(w, h)] = const.tile([P, 1024], U32, name="codes_%s%d" % (w, h), align_bytes=64)
+            scales_w[(w, h)] = const.tile([P, 1024], U8, name="scales_%s%d" % (w, h), align_bytes=64)
 
-        def quant_weight(w, h, pieces):
-            codes = const.tile([P, 1024], U32, name="codes_%s%d" % (w, h), align_bytes=64)
-            scales = const.tile([P, 1024], U8, name="scales_%s%d" % (w, h), align_bytes=64)
-            codes_w[(w, h)] = codes
-            scales_w[(w, h)] = scales
+        def prep_block(w, h, i, engines):
+            gi, e = block_order(w)[i]
+            evacuate(
+                transpose_block(w_raw[(w, h)][:, gi, e, :].bitcast(F32)),
+                grouped_w[(w, h)][:].bitcast(F32)[:, :, i * P : (i + 1) * P, :],
+                engines,
+            )
+
+        def quant_weight(w, h, lo, hi):
             flat = grouped_w[(w, h)][:].rearrange("p g n j -> p (g n j)")
-            step = 1024 // pieces
-            for i in range(pieces):
-                lo = i * step
-                hi = lo + step
-                nc.vector.quantize_mx(
-                    out=codes[:, lo:hi].bitcast(E5X4), scales=scales[:, lo:hi], in_=flat[:, 4 * lo : 4 * hi]
-                )
+            nc.vector.quantize_mx(
+                out=codes_w[(w, h)][:, lo:hi].bitcast(E5X4),
+                scales=scales_w[(w, h)][:, lo:hi],
+                in_=flat[:, 4 * lo : 4 * hi],
+            )
 
         def project(w, m, h):
             acc = psum.tile([P, 512], F32, name="acc", tag="bank")
@@ -209,9 +202,9 @@ def tile_attention_pa_kernel(tc, emb, W1, W2, W3, out_0, out_1, out_2):
 
         def rope_products(acc, h, prod, slot):
             nc.vector.tensor_tensor(
-                out=prod[:, slot, :, :].rearrange("p e (x r) -> p (e x) r", r=2),
-                in0=acc[:].unsqueeze(2).to_broadcast([P, 512, 2]),
-                in1=table[:, h, :, :, :].rearrange("p e x r -> p (e x) r"),
+                out=prod[:, slot, :, :].rearrange("p s (x r) -> p s x r", r=2),
+                in0=acc[:].rearrange("p (s x) -> p s x", s=2).unsqueeze(3).to_broadcast([P, 2, 256, 2]),
+                in1=trig[:, :, :, h * 256 : (h + 1) * 256].rearrange("p s r x -> p s x r"),
                 op=ALU.mult,
             )
 
@@ -225,66 +218,83 @@ def tile_attention_pa_kernel(tc, emb, W1, W2, W3, out_0, out_1, out_2):
                     in_=y[:],
                 )
 
-        def rope_sum_store(prod, pair):
+        def rope_sum_store(prod, pair, gcols):
             y = ypool.tile([P, 2, 512], F32, name="y", tag="y")
-            nc.gpsimd.tensor_tensor(out=y[:], in0=prod[:, :, 0, :], in1=prod[:, :, 1, :], op=ALU.add)
+            vfirst = gcols - 8
+            nc.vector.tensor_tensor(
+                out=y[:, :, vfirst:512], in0=prod[:, :, 0, vfirst:512], in1=prod[:, :, 1, vfirst:512], op=ALU.add
+            )
+            nc.gpsimd.tensor_tensor(
+                out=y[:, :, 0:gcols], in0=prod[:, :, 0, 0:gcols], in1=prod[:, :, 1, 0:gcols], op=ALU.add
+            )
             store_pair(y, pair)
 
-        prep_emb(0, "S")
-        build_trig()
-        build_table(0)
-        build_table(1)
+        prep_emb(0, "V")
+        build_trig(0)
+        open_weight("Q", 0)
+        prep_block("Q", 0, 0, "V")
         quant_emb(0, 1)
-        prep_weight("Q", 0, "VVVS")
+        prep_block("Q", 0, 1, "S")
+        quant_weight("Q", 0, 0, 256)
+        quant_weight("Q", 0, 512, 768)
+        prep_block("Q", 0, 2, "S")
+        prep_block("Q", 0, 3, "VS")
+        quant_weight("Q", 0, 256, 384)
+        quant_weight("Q", 0, 384, 512)
+        quant_weight("Q", 0, 768, 896)
+        quant_weight("Q", 0, 896, 1024)
         prep_emb(1, "S")
         prep_emb(2, "S")
-        prep_emb(3, "S")
-        quant_weight("Q", 0, 2)
         quant_emb(1, 1)
 
-        pairs = [
-            (("Q", 0, 0), ("Q", 1, 0)),
-            (("Q", 2, 0), ("Q", 3, 0)),
-            (("Q", 0, 1), ("Q", 1, 1)),
-            (("Q", 2, 1), ("Q", 3, 1)),
-        ]
-        pairs.extend([(("Q", m, 0), ("Q", m, 1)) for m in range(4, 8)])
+        pairs = [(("Q", m, h), ("Q", m + 1, h)) for h in range(2) for m in range(0, 8, 2)]
         pairs.extend([(("K", m, 0), ("K", m, 1)) for m in range(8)])
-        runs = [("Q", 1), ("E", 4), ("V", 0), ("V", 1), ("K", 0), ("K", 1)]
+        chunks = [("Q", 1), ("V", 0), ("V", 1), ("K", 0), ("K", 1)]
+
+        first = project("Q", 0, 0)
+        prep_emb(3, "S")
+        prep_emb(4, "S")
+        accs = [first, project("Q", 1, 0)]
+        waiting = {}
+
+        def sum_waiting():
+            prod_w, pair_w, j_w = waiting[0]
+            rope_sum_store(prod_w, pair_w, GCOLS_BY_STEP.get(j_w, GCOLS))
 
         for j in range(16):
             pair = pairs[j]
-            accs = [project(w, m, h) for (w, m, h) in pair]
+            prod = tpool.tile([P, 2, 2, 512], F32, name="prod", tag="prod")
+            rope_products(accs[0], pair[0][2], prod, 0)
+            if j == 0:
+                quant_emb(2, 1)
+                quant_emb(3, 1)
+            elif j == 1:
+                quant_emb(4, 1)
+                sum_waiting()
+                quant_emb(5, 1)
+            elif j == 2:
+                quant_emb(6, 2)
+                sum_waiting()
+            else:
+                if j - 3 < 5:
+                    quant_weight(chunks[j - 3][0], chunks[j - 3][1], 0, 1024)
+                sum_waiting()
+            second = accs[1]
+            if j < 15:
+                accs = [project(w, m, h) for (w, m, h) in pairs[j + 1]]
             vaccs = []
-            if j < 6:
-                if runs[j][0] == "E":
-                    for m in range(4, 8):
-                        prep_emb(m, "S")
-                else:
-                    prep_weight(runs[j][0], runs[j][1], "SSSS")
+            if j == 0:
+                for m in range(5, 8):
+                    prep_emb(m, "S")
+                build_trig(1)
+            elif j <= 5:
+                open_weight(chunks[j - 1][0], chunks[j - 1][1])
+                for i in range(4):
+                    prep_block(chunks[j - 1][0], chunks[j - 1][1], i, "S")
             elif j < 14:
                 vaccs = [project("V", j - 6, h) for h in range(2)]
-            prod = tpool.tile([P, 2, 2, 512], F32, name="prod", tag="prod")
-            if j == 15:
-                y = ypool.tile([P, 2, 512], F32, name="y", tag="y")
-                for slot in range(2):
-                    (w, m, h) = pair[slot]
-                    rope_products(accs[slot], h, prod, slot)
-                    nc.vector.tensor_tensor(
-                        out=y[:, slot, :], in0=prod[:, slot, 0, :], in1=prod[:, slot, 1, :], op=ALU.add
-                    )
-                    nc.sync.dma_start(out=outs[w][m * P : (m + 1) * P, h * 512 : (h + 1) * 512], in_=y[:, slot, :])
-            else:
-                rope_products(accs[0], pair[0][2], prod, 0)
-                if j == 0:
-                    quant_emb(2, 2)
-                rope_products(accs[1], pair[1][2], prod, 1)
-                if 1 <= j <= 6:
-                    if runs[j - 1][0] == "E":
-                        quant_emb(4, 4)
-                    else:
-                        quant_weight(runs[j - 1][0], runs[j - 1][1], 2 if j == 1 else 1)
-                rope_sum_store(prod, pair)
+            rope_products(second, pair[1][2], prod, 1)
+            waiting[0] = (prod, pair, j)
             if vaccs:
                 yv = vpool.tile([P, 2, 512], F32, name="yv", tag="yv")
                 for h in range(2):
@@ -294,3 +304,10 @@ def tile_attention_pa_kernel(tc, emb, W1, W2, W3, out_0, out_1, out_2):
                     )
                 mv = j - 6
                 nc.scalar.dma_start(out=outs["V"][mv * P : (mv + 1) * P, :], in_=yv[:].rearrange("p b c -> p (b c)"))
+
+        prod, pair, j = waiting[0]
+        y = ypool.tile([P, 2, 512], F32, name="y", tag="y")
+        for slot in range(2):
+            (w, m, h) = pair[slot]
+            nc.vector.tensor_tensor(out=y[:, slot, :], in0=prod[:, slot, 0, :], in1=prod[:, slot, 1, :], op=ALU.add)
+            nc.sync.dma_start(out=outs[w][m * P : (m + 1) * P, h * 512 : (h + 1) * 512], in_=y[:, slot, :])

@@ -39,6 +39,9 @@ def tile_attention_pa_kernel(tc, emb, W1, W2, W3, out_0, out_1, out_2):
         vpool = ctx.enter_context(tc.tile_pool(name="vpool", bufs=3))
         psum = ctx.enter_context(tc.psum_pool(name="psum", bufs=8))
 
+        wz = const.tile([P, 512], BF16, name="wz")
+        nc.gpsimd.memset(wz[:], 0.0)
+
         emb_words = {}
         w_raw = {}
 
@@ -91,40 +94,53 @@ def tile_attention_pa_kernel(tc, emb, W1, W2, W3, out_0, out_1, out_2):
         make_identity(nc, ident[:])
 
         ratio = 10000.0 ** (-1.0 / 64.0)
-        gtab = const.tile([P, 64], F32, name="gtab")
-        nc.vector.memset(gtab[:, 0:1], 1.0)
-        for k in range(6):
+        powers = const.tile([P, 2, 8], F32, name="powers")
+        nc.vector.memset(powers[:, :, 0:1], 1.0)
+        for k in range(3):
             n = 1 << k
-            nc.vector.tensor_scalar_mul(out=gtab[:, n : 2 * n], in0=gtab[:, 0:n], scalar1=ratio ** n)
-        turns = const.tile([P, 8, 64], F32, name="turns")
+            nc.vector.tensor_scalar_mul(out=powers[:, 0, n : 2 * n], in0=powers[:, 0, 0:n], scalar1=ratio ** (8 * n))
+            nc.vector.tensor_scalar_mul(out=powers[:, 1, n : 2 * n], in0=powers[:, 1, 0:n], scalar1=ratio ** n)
+        gtab = const.tile([P, 8, 8], F32, name="gtab")
         nc.vector.scalar_tensor_tensor(
-            out=turns[:],
-            in0=pos_i[:].unsqueeze(2).to_broadcast([P, 8, 64]),
+            out=gtab[:],
+            in0=powers[:, 0, :].unsqueeze(2).to_broadcast([P, 8, 8]),
             scalar=1.0 / (2.0 * PI),
-            in1=gtab[:].unsqueeze(1).to_broadcast([P, 8, 64]),
+            in1=powers[:, 1, :].unsqueeze(1).to_broadcast([P, 8, 8]),
             op0=ALU.mult,
             op1=ALU.mult,
         )
+        gtab_flat = gtab[:].rearrange("p a b -> p (a b)")
+        turns = const.tile([P, 8, 64], F32, name="turns")
         turns_flat = turns[:].rearrange("p c i -> p (c i)")
         whole_i = const.tile([P, 512], I32, name="whole_i")
-        nc.vector.tensor_copy(out=whole_i[:], in_=turns_flat)
         frac = const.tile([P, 512], F32, name="frac")
-        nc.vector.tensor_tensor(out=frac[:], in0=turns_flat, in1=whole_i[:], op=ALU.subtract)
-        nfrac = const.tile([P, 512], F32, name="nfrac")
-        nc.vector.scalar_tensor_tensor(
-            out=nfrac[:], in0=frac[:], scalar=0.5, in1=frac[:], op0=ALU.is_ge, op1=ALU.subtract
-        )
+        halves = [slice(0, 256), slice(256, 512)]
+        for h in range(2):
+            nc.vector.tensor_tensor(
+                out=turns[:, 4 * h : 4 * h + 4, :],
+                in0=pos_i[:, 4 * h : 4 * h + 4].unsqueeze(2).to_broadcast([P, 4, 64]),
+                in1=gtab_flat.unsqueeze(1).to_broadcast([P, 4, 64]),
+                op=ALU.mult,
+            )
+        for h in range(2):
+            nc.vector.tensor_copy(out=whole_i[:, halves[h]], in_=turns_flat[:, halves[h]])
+        for h in range(2):
+            nc.vector.tensor_tensor(
+                out=frac[:, halves[h]], in0=turns_flat[:, halves[h]], in1=whole_i[:, halves[h]], op=ALU.subtract
+            )
         absn = const.tile([P, 512], F32, name="absn")
         trig = const.tile([P, 2, 2, 512], F32, name="trig")
 
         def build_trig(h):
-            cols = slice(h * 256, (h + 1) * 256)
+            cols = halves[h]
             two_pi = 2.0 * PI
-            nc.scalar.activation(out=absn[:, cols], in_=nfrac[:, cols], func=ACT.Abs)
-            nc.scalar.activation(out=trig[:, 0, 0, cols], in_=nfrac[:, cols], func=ACT.Sin, scale=two_pi)
+            nc.scalar.activation(out=trig[:, 1, 1, cols], in_=frac[:, cols], func=ACT.Sin, scale=two_pi)
+            nc.scalar.activation(out=absn[:, cols], in_=frac[:, cols], func=ACT.Abs)
             nc.scalar.activation(out=trig[:, 0, 1, cols], in_=absn[:, cols], func=ACT.Sin, scale=-two_pi, bias=0.5 * PI)
-            nc.scalar.activation(out=trig[:, 1, 0, cols], in_=absn[:, cols], func=ACT.Sin, scale=-two_pi, bias=0.5 * PI)
-            nc.scalar.activation(out=trig[:, 1, 1, cols], in_=nfrac[:, cols], func=ACT.Sin, scale=-two_pi)
+            nc.gpsimd.tensor_scalar(
+                out=trig[:, 0, 0, cols], in0=trig[:, 1, 1, cols], scalar1=-1.0, scalar2=0.0, op0=ALU.mult, op1=ALU.add
+            )
+            nc.gpsimd.tensor_copy(out=trig[:, 1, 0, cols], in_=trig[:, 0, 1, cols])
 
         grouped_e = const.tile([P, 8, 2, P, 4], BF16, name="grouped_e", align_bytes=64)
         grouped_e_flat = grouped_e[:].rearrange("p m g r j -> p (m g r j)")
@@ -134,8 +150,12 @@ def tile_attention_pa_kernel(tc, emb, W1, W2, W3, out_0, out_1, out_2):
         scales_w = {}
         grouped_w = {}
 
-        def transpose_block(words):
+        def transpose_block(words, warm=0):
             bank = psum.tile([P, 2, 2, P], F32, name="tp", tag="bank")
+            for i in range(warm):
+                nc.tensor.matmul(
+                    out=bank[:].rearrange("p g u r -> p (g u r)"), lhsT=wz[:, 0:P], rhs=wz[:], start=True, stop=True
+                )
             for g in range(2):
                 for u in range(2):
                     nc.tensor.transpose(bank[:, g, u, :], words[:, 256 * g + u : 256 * (g + 1) : 2], ident[:])
@@ -154,8 +174,8 @@ def tile_attention_pa_kernel(tc, emb, W1, W2, W3, out_0, out_1, out_2):
                 for g in range(2):
                     copy_out(engines[g], dst[:, g, :, :], bank[:, g, :, :].rearrange("p u r -> p r u"))
 
-        def prep_emb(m, engines):
-            evacuate(transpose_block(emb_words[m]), grouped_e[:, m, :, :, :].bitcast(F32), engines)
+        def prep_emb(m, engines, warm=0):
+            evacuate(transpose_block(emb_words[m], warm), grouped_e[:, m, :, :, :].bitcast(F32), engines)
 
         def quant_emb(first, count):
             lo = first * 256
@@ -169,10 +189,10 @@ def tile_attention_pa_kernel(tc, emb, W1, W2, W3, out_0, out_1, out_2):
             codes_w[(w, h)] = const.tile([P, 1024], U32, name="codes_%s%d" % (w, h), align_bytes=64)
             scales_w[(w, h)] = const.tile([P, 1024], U8, name="scales_%s%d" % (w, h), align_bytes=64)
 
-        def prep_block(w, h, i, engines):
+        def prep_block(w, h, i, engines, warm=0):
             gi, e = block_order(w)[i]
             evacuate(
-                transpose_block(w_raw[(w, h)][:, gi, e, :].bitcast(F32)),
+                transpose_block(w_raw[(w, h)][:, gi, e, :].bitcast(F32), warm),
                 grouped_w[(w, h)][:].bitcast(F32)[:, :, i * P : (i + 1) * P, :],
                 engines,
             )
@@ -229,22 +249,25 @@ def tile_attention_pa_kernel(tc, emb, W1, W2, W3, out_0, out_1, out_2):
             )
             store_pair(y, pair)
 
-        prep_emb(0, "V")
+        def quant_block(w, h, i):
+            for g in range(2):
+                quant_weight(w, h, g * 512 + i * P, g * 512 + (i + 1) * P)
+
         build_trig(0)
+        prep_emb(0, "V", 3)
         open_weight("Q", 0)
-        prep_block("Q", 0, 0, "V")
+        prep_block("Q", 0, 0, "V", 0)
         quant_emb(0, 1)
-        prep_block("Q", 0, 1, "S")
-        quant_weight("Q", 0, 0, 256)
-        quant_weight("Q", 0, 512, 768)
-        prep_block("Q", 0, 2, "S")
-        prep_block("Q", 0, 3, "VS")
-        quant_weight("Q", 0, 256, 384)
-        quant_weight("Q", 0, 384, 512)
-        quant_weight("Q", 0, 768, 896)
-        quant_weight("Q", 0, 896, 1024)
-        prep_emb(1, "S")
-        prep_emb(2, "S")
+        quant_block("Q", 0, 0)
+        prep_block("Q", 0, 1, "S", 1)
+        prep_block("Q", 0, 2, "S", 0)
+        quant_block("Q", 0, 1)
+        prep_block("Q", 0, 3, "VS", 1)
+        for g in range(2):
+            for i in range(2, 4):
+                quant_weight("Q", 0, g * 512 + i * P, g * 512 + (i + 1) * P)
+        prep_emb(1, "S", 0)
+        prep_emb(2, "S", 1)
         quant_emb(1, 1)
 
         pairs = [(("Q", m, h), ("Q", m + 1, h)) for h in range(2) for m in range(0, 8, 2)]

@@ -254,19 +254,19 @@ def tile_attention_pa_kernel(tc, emb, W1, W2, W3, out_0, out_1, out_2):
                 quant_weight(w, h, g * 512 + i * P, g * 512 + (i + 1) * P)
 
         build_trig(0)
-        prep_emb(0, "V", 3)
+        prep_emb(0, "V", 4)
         open_weight("Q", 0)
-        prep_block("Q", 0, 0, "V", 0)
+        prep_block("Q", 0, 0, "V", 1)
         quant_emb(0, 1)
         quant_block("Q", 0, 0)
         prep_block("Q", 0, 1, "S", 1)
-        prep_block("Q", 0, 2, "S", 0)
+        prep_block("Q", 0, 2, "S", 1)
         quant_block("Q", 0, 1)
         prep_block("Q", 0, 3, "VS", 1)
         for g in range(2):
             for i in range(2, 4):
                 quant_weight("Q", 0, g * 512 + i * P, g * 512 + (i + 1) * P)
-        prep_emb(1, "S", 0)
+        prep_emb(1, "S", 1)
         prep_emb(2, "S", 1)
         quant_emb(1, 1)
 
@@ -304,7 +304,9 @@ def tile_attention_pa_kernel(tc, emb, W1, W2, W3, out_0, out_1, out_2):
                 sum_waiting()
             second = accs[1]
             if j < 15:
-                accs = [project(w, m, h) for (w, m, h) in pairs[j + 1]]
+                accs = [project(pairs[j + 1][0][0], pairs[j + 1][0][1], pairs[j + 1][0][2])]
+                if j < 1 or j > 5:
+                    accs.append(project(pairs[j + 1][1][0], pairs[j + 1][1][1], pairs[j + 1][1][2]))
             vaccs = []
             if j == 0:
                 for m in range(5, 8):
@@ -312,7 +314,10 @@ def tile_attention_pa_kernel(tc, emb, W1, W2, W3, out_0, out_1, out_2):
                 build_trig(1)
             elif j <= 5:
                 open_weight(chunks[j - 1][0], chunks[j - 1][1])
-                for i in range(4):
+                for i in range(2):
+                    prep_block(chunks[j - 1][0], chunks[j - 1][1], i, "S")
+                accs.append(project(pairs[j + 1][1][0], pairs[j + 1][1][1], pairs[j + 1][1][2]))
+                for i in range(2, 4):
                     prep_block(chunks[j - 1][0], chunks[j - 1][1], i, "S")
             elif j < 14:
                 vaccs = [project("V", j - 6, h) for h in range(2)]

@@ -16,8 +16,8 @@ PI = 3.141592653589793
 P = 128
 K = 1024
 FLOPS = 2 * 1024 * 1024 * 3072
-GCOLS = 416
-GCOLS_BY_STEP = {14: 208}
+GCOLS = 336
+GCOLS_BY_STEP = {14: 168}
 
 
 def tile_attention_pa_kernel(tc, emb, W1, W2, W3, out_0, out_1, out_2):
@@ -137,10 +137,14 @@ def tile_attention_pa_kernel(tc, emb, W1, W2, W3, out_0, out_1, out_2):
             nc.scalar.activation(out=trig[:, 1, 1, cols], in_=frac[:, cols], func=ACT.Sin, scale=two_pi)
             nc.scalar.activation(out=absn[:, cols], in_=frac[:, cols], func=ACT.Abs)
             nc.scalar.activation(out=trig[:, 0, 1, cols], in_=absn[:, cols], func=ACT.Sin, scale=-two_pi, bias=0.5 * PI)
-            nc.gpsimd.tensor_scalar(
-                out=trig[:, 0, 0, cols], in0=trig[:, 1, 1, cols], scalar1=-1.0, scalar2=0.0, op0=ALU.mult, op1=ALU.add
-            )
-            nc.gpsimd.tensor_copy(out=trig[:, 1, 0, cols], in_=trig[:, 0, 1, cols])
+            if h == 0:
+                nc.gpsimd.tensor_scalar(
+                    out=trig[:, 0, 0, cols], in0=trig[:, 1, 1, cols], scalar1=-1.0, scalar2=0.0, op0=ALU.mult, op1=ALU.add
+                )
+                nc.gpsimd.tensor_copy(out=trig[:, 1, 0, cols], in_=trig[:, 0, 1, cols])
+            else:
+                nc.scalar.activation(out=trig[:, 0, 0, cols], in_=frac[:, cols], func=ACT.Sin, scale=-two_pi)
+                nc.scalar.activation(out=trig[:, 1, 0, cols], in_=absn[:, cols], func=ACT.Sin, scale=-two_pi, bias=0.5 * PI)
 
         grouped_e = const.tile([P, 8, 2, P, 4], BF16, name="grouped_e", align_bytes=64)
         grouped_e_flat = grouped_e[:].rearrange("p m g r j -> p (m g r j)")

@@ -16,8 +16,8 @@ PI = 3.141592653589793
 P = 128
 K = 1024
 FLOPS = 2 * 1024 * 1024 * 3072
-GCOLS = 336
-GCOLS_BY_STEP = {14: 168}
+GCOLS = 416
+GCOLS_BY_STEP = {14: 208}
 
 
 def tile_attention_pa_kernel(tc, emb, W1, W2, W3, out_0, out_1, out_2):

@@ -35,7 +35,7 @@ def tile_attention_pa_kernel(tc, emb, W1, W2, W3, out_0, out_1, out_2):
         const = ctx.enter_context(tc.tile_pool(name="const", bufs=1))
         grp = ctx.enter_context(tc.tile_pool(name="grp", bufs=3))
         tpool = ctx.enter_context(tc.tile_pool(name="tpool", bufs=4))
-        ypool = ctx.enter_context(tc.tile_pool(name="ypool", bufs=3))
+        ypool = ctx.enter_context(tc.tile_pool(name="ypool", bufs=5))
         vpool = ctx.enter_context(tc.tile_pool(name="vpool", bufs=3))
         psum = ctx.enter_context(tc.psum_pool(name="psum", bufs=8))
 

@@ -39,9 +39,6 @@ def tile_attention_pa_kernel(tc, emb, W1, W2, W3, out_0, out_1, out_2):
         vpool = ctx.enter_context(tc.tile_pool(name="vpool", bufs=3))
         psum = ctx.enter_context(tc.psum_pool(name="psum", bufs=8))
 
-        wz = const.tile([P, 512], BF16, name="wz")
-        nc.gpsimd.memset(wz[:], 0.0)
-
         emb_words = {}
         w_raw = {}
 
@@ -156,10 +153,6 @@ def tile_attention_pa_kernel(tc, emb, W1, W2, W3, out_0, out_1, out_2):
 
         def transpose_block(words, warm=0):
             bank = psum.tile([P, 2, 2, P], F32, name="tp", tag="bank")
-            for i in range(warm):
-                nc.tensor.matmul(
-                    out=bank[:].rearrange("p g u r -> p (g u r)"), lhsT=wz[:, 0:P], rhs=wz[:], start=True, stop=True
-                )
             for g in range(2):
                 for u in range(2):
                     nc.tensor.transpose(bank[:, g, u, :], words[:, 256 * g + u : 256 * (g + 1) : 2], ident[:])
@@ -258,20 +251,20 @@ def tile_attention_pa_kernel(tc, emb, W1, W2, W3, out_0, out_1, out_2):
                 quant_weight(w, h, g * 512 + i * P, g * 512 + (i + 1) * P)
 
         build_trig(0)
-        prep_emb(0, "V", 4)
+        prep_emb(0, "V", 0)
         open_weight("Q", 0)
-        prep_block("Q", 0, 0, "V", 1)
+        prep_block("Q", 0, 0, "V", 0)
         quant_emb(0, 1)
         quant_block("Q", 0, 0)
-        prep_block("Q", 0, 1, "S", 1)
-        prep_block("Q", 0, 2, "S", 1)
+        prep_block("Q", 0, 1, "S", 0)
+        prep_block("Q", 0, 2, "S", 0)
         quant_block("Q", 0, 1)
-        prep_block("Q", 0, 3, "VS", 1)
+        prep_block("Q", 0, 3, "VS", 0)
         for g in range(2):
             for i in range(2, 4):
                 quant_weight("Q", 0, g * 512 + i * P, g * 512 + (i + 1) * P)
-        prep_emb(1, "S", 1)
-        prep_emb(2, "S", 1)
+        prep_emb(1, "S", 0)
+        prep_emb(2, "S", 0)
         quant_emb(1, 1)
 
         pairs = [(("Q", m, h), ("Q", m + 1, h)) for h in range(2) for m in range(0, 8, 2)]

@@ -17,7 +17,7 @@ P = 128
 K = 1024
 FLOPS = 2 * 1024 * 1024 * 3072
 GCOLS = 416
-GCOLS_BY_STEP = {14: 208}
+GCOLS_BY_STEP = {14: 128}
 
 
 def tile_attention_pa_kernel(tc, emb, W1, W2, W3, out_0, out_1, out_2):
@@ -134,14 +134,8 @@ def tile_attention_pa_kernel(tc, emb, W1, W2, W3, out_0, out_1, out_2):
             nc.scalar.activation(out=trig[:, 1, 1, cols], in_=frac[:, cols], func=ACT.Sin, scale=two_pi)
             nc.scalar.activation(out=absn[:, cols], in_=frac[:, cols], func=ACT.Abs)
             nc.scalar.activation(out=trig[:, 0, 1, cols], in_=absn[:, cols], func=ACT.Sin, scale=-two_pi, bias=0.5 * PI)
-            if h == 0:
-                nc.gpsimd.tensor_scalar(
-                    out=trig[:, 0, 0, cols], in0=trig[:, 1, 1, cols], scalar1=-1.0, scalar2=0.0, op0=ALU.mult, op1=ALU.add
-                )
-                nc.gpsimd.tensor_copy(out=trig[:, 1, 0, cols], in_=trig[:, 0, 1, cols])
-            else:
-                nc.scalar.activation(out=trig[:, 0, 0, cols], in_=frac[:, cols], func=ACT.Sin, scale=-two_pi)
-                nc.scalar.activation(out=trig[:, 1, 0, cols], in_=absn[:, cols], func=ACT.Sin, scale=-two_pi, bias=0.5 * PI)
+            nc.scalar.activation(out=trig[:, 0, 0, cols], in_=frac[:, cols], func=ACT.Sin, scale=-two_pi)
+            nc.scalar.activation(out=trig[:, 1, 0, cols], in_=absn[:, cols], func=ACT.Sin, scale=-two_pi, bias=0.5 * PI)
 
         grouped_e = const.tile([P, 8, 2, P, 4], BF16, name="grouped_e", align_bytes=64)
         grouped_e_flat = grouped_e[:].rearrange("p m g r j -> p (m g r j)")
@@ -301,9 +295,7 @@ def tile_attention_pa_kernel(tc, emb, W1, W2, W3, out_0, out_1, out_2):
                 sum_waiting()
             second = accs[1]
             if j < 15:
-                accs = [project(pairs[j + 1][0][0], pairs[j + 1][0][1], pairs[j + 1][0][2])]
-                if j < 1 or j > 5:
-                    accs.append(project(pairs[j + 1][1][0], pairs[j + 1][1][1], pairs[j + 1][1][2]))
+                accs = [project(w, m, h) for (w, m, h) in pairs[j + 1]]
             vaccs = []
             if j == 0:
                 for m in range(5, 8):
@@ -311,10 +303,7 @@ def tile_attention_pa_kernel(tc, emb, W1, W2, W3, out_0, out_1, out_2):
                 build_trig(1)
             elif j <= 5:
                 open_weight(chunks[j - 1][0], chunks[j - 1][1])
-                for i in range(2):
-                    prep_block(chunks[j - 1][0], chunks[j - 1][1], i, "S")
-                accs.append(project(pairs[j + 1][1][0], pairs[j + 1][1][1], pairs[j + 1][1][2]))
-                for i in range(2, 4):
+                for i in range(4):
                     prep_block(chunks[j - 1][0], chunks[j - 1][1], i, "S")
             elif j < 14:
                 vaccs = [project("V", j - 6, h) for h in range(2)]
@@ -332,7 +321,9 @@ def tile_attention_pa_kernel(tc, emb, W1, W2, W3, out_0, out_1, out_2):
 
         prod, pair, j = waiting[0]
         y = ypool.tile([P, 2, 512], F32, name="y", tag="y")
-        for slot in range(2):
+        for slot, lo, hi in ((0, 0, 512), (1, 0, 256), (1, 256, 512)):
             (w, m, h) = pair[slot]
-            nc.vector.tensor_tensor(out=y[:, slot, :], in0=prod[:, slot, 0, :], in1=prod[:, slot, 1, :], op=ALU.add)
-            nc.sync.dma_start(out=outs[w][m * P : (m + 1) * P, h * 512 : (h + 1) * 512], in_=y[:, slot, :])
+            nc.vector.tensor_tensor(
+                out=y[:, slot, lo:hi], in0=prod[:, slot, 0, lo:hi], in1=prod[:, slot, 1, lo:hi], op=ALU.add
+            )
+            nc.sync.dma_start(out=outs[w][m * P : (m + 1) * P, h * 512 + lo : h * 512 + hi], in_=y[:, slot, lo:hi])

@@ -17,7 +17,7 @@ P = 128
 K = 1024
 FLOPS = 2 * 1024 * 1024 * 3072
 GCOLS = 416
-GCOLS_BY_STEP = {14: 128}
+GCOLS_BY_STEP = {j: 128 if j == 14 else 512 for j in range(7, 15)}
 
 
 def tile_attention_pa_kernel(tc, emb, W1, W2, W3, out_0, out_1, out_2):
@@ -231,10 +231,11 @@ def tile_attention_pa_kernel(tc, emb, W1, W2, W3, out_0, out_1, out_2):
 
         def rope_sum_store(prod, pair, gcols):
             y = ypool.tile([P, 2, 512], F32, name="y", tag="y")
-            vfirst = gcols - 8
-            nc.vector.tensor_tensor(
-                out=y[:, :, vfirst:512], in0=prod[:, :, 0, vfirst:512], in1=prod[:, :, 1, vfirst:512], op=ALU.add
-            )
+            if gcols < 512:
+                vfirst = gcols - 8
+                nc.vector.tensor_tensor(
+                    out=y[:, :, vfirst:512], in0=prod[:, :, 0, vfirst:512], in1=prod[:, :, 1, vfirst:512], op=ALU.add
+                )
             nc.gpsimd.tensor_tensor(
                 out=y[:, :, 0:gcols], in0=prod[:, :, 0, 0:gcols], in1=prod[:, :, 1, 0:gcols], op=ALU.add
             )

from contextlib import ExitStack

import concourse.mybir as mybir
from concourse.masks import make_identity

F32 = mybir.dt.float32
BF16 = mybir.dt.bfloat16
I32 = mybir.dt.int32
U32 = mybir.dt.uint32
U8 = mybir.dt.uint8
E5X4 = mybir.dt.float8_e5m2_x4
ALU = mybir.AluOpType
ACT = mybir.ActivationFunctionType

PI = 3.141592653589793
P = 128
K = 1024
FLOPS = 2 * 1024 * 1024 * 3072
GCOLS = 416
GCOLS_BY_STEP = {j: 128 if j == 14 else 512 for j in range(7, 15)}


def tile_attention_pa_kernel(tc, emb, W1, W2, W3, out_0, out_1, out_2):
    nc = tc.nc
    emb_rows = emb.rearrange("b s e -> (b s) e")
    weights = {"Q": W1, "K": W2, "V": W3}
    outs = {
        "Q": out_0.rearrange("b h (s c) d -> (b h s) (c d)", c=8),
        "K": out_1.rearrange("b h (s c) d -> (b h s) (c d)", c=8),
        "V": out_2.rearrange("b h (s c) d -> (b h s) (c d)", c=8),
    }

    with ExitStack() as ctx:
        ctx.enter_context(tc.manual_schedule())
        const = ctx.enter_context(tc.tile_pool(name="const", bufs=1))
        grp = ctx.enter_context(tc.tile_pool(name="grp", bufs=3))
        tpool = ctx.enter_context(tc.tile_pool(name="tpool", bufs=4))
        ypool = ctx.enter_context(tc.tile_pool(name="ypool", bufs=5))
        vpool = ctx.enter_context(tc.tile_pool(name="vpool", bufs=3))
        psum = ctx.enter_context(tc.psum_pool(name="psum", bufs=8))

        emb_words = {}
        w_raw = {}

        def load_emb(first, count):
            raw = const.tile([P, count, K], BF16, name="raw_e%d" % first)
            nc.sync.dma_start(
                out=raw[:],
                in_=emb_rows[first * P : (first + count) * P, :].rearrange("(m p) k -> p m k", p=P),
            )
            for i in range(count):
                emb_words[first + i] = raw[:, i, :].bitcast(F32)

        def block_order(w):
            first_e = 0 if w == "V" else 1
            return [(0, first_e), (1, first_e), (0, 1 - first_e), (1, 1 - first_e)]

        def load_weight(w, h, by_block):
            raw = const.tile([P, 2, 2, K], BF16, name="raw_%s%d" % (w, h))
            rows = weights[w][h * 512 : (h + 1) * 512, :]
            if by_block:
                view = rows.rearrange("(gi p e) k -> p gi e k", gi=2, e=2)
                for gi, e in block_order(w):
                    nc.sync.dma_start(out=raw[:, gi, e, :], in_=view[:, gi, e, :])
            else:
                nc.sync.dma_start(
                    out=raw[:].rearrange("p gi e k -> p gi (e k)"),
                    in_=rows.rearrange("(gi p e) k -> p gi (e k)", gi=2, e=2),
                )
            w_raw[(w, h)] = raw

        load_emb(0, 1)
        load_weight("Q", 0, True)
        for m in range(1, 8):
            load_emb(m, 1)
        load_weight("Q", 1, False)
        load_weight("V", 0, False)
        load_weight("V", 1, False)
        load_weight("K", 0, False)
        load_weight("K", 1, False)

        zero = const.tile([P, 1], F32, name="zero")
        warm = const.tile([P, 1], F32, name="warm")
        nc.vector.memset(zero[:], 0.0)
        nc.scalar.activation(out=warm[:], in_=zero[:], func=ACT.Sin)

        pos_i = const.tile([P, 8], I32, name="pos_i")
        nc.gpsimd.iota(pos_i[0:64, :], pattern=[[1, 8]], base=0, channel_multiplier=8)
        nc.gpsimd.iota(pos_i[64:128, :], pattern=[[1, 8]], base=0, channel_multiplier=8)
        ident = const.tile([P, P], F32, name="ident")
        make_identity(nc, ident[:])

        ratio = 10000.0 ** (-1.0 / 64.0)
        powers = const.tile([P, 2, 8], F32, name="powers")
        nc.vector.memset(powers[:, :, 0:1], 1.0)
        for k in range(3):
            n = 1 << k
            nc.vector.tensor_scalar_mul(out=powers[:, 0, n : 2 * n], in0=powers[:, 0, 0:n], scalar1=ratio ** (8 * n))
            nc.vector.tensor_scalar_mul(out=powers[:, 1, n : 2 * n], in0=powers[:, 1, 0:n], scalar1=ratio ** n)
        gtab = const.tile([P, 8, 8], F32, name="gtab")
        nc.vector.scalar_tensor_tensor(
            out=gtab[:],
            in0=powers[:, 0, :].unsqueeze(2).to_broadcast([P, 8, 8]),
            scalar=1.0 / (2.0 * PI),
            in1=powers[:, 1, :].unsqueeze(1).to_broadcast([P, 8, 8]),
            op0=ALU.mult,
            op1=ALU.mult,
        )
        gtab_flat = gtab[:].rearrange("p a b -> p (a b)")
        turns = const.tile([P, 8, 64], F32, name="turns")
        turns_flat = turns[:].rearrange("p c i -> p (c i)")
        whole_i = const.tile([P, 512], I32, name="whole_i")
        frac = const.tile([P, 512], F32, name="frac")
        halves = [slice(0, 256), slice(256, 512)]
        for h in range(2):
            nc.vector.tensor_tensor(
                out=turns[:, 4 * h : 4 * h + 4, :],
                in0=pos_i[:, 4 * h : 4 * h + 4].unsqueeze(2).to_broadcast([P, 4, 64]),
                in1=gtab_flat.unsqueeze(1).to_broadcast([P, 4, 64]),
                op=ALU.mult,
            )
        for h in range(2):
            nc.vector.tensor_copy(out=whole_i[:, halves[h]], in_=turns_flat[:, halves[h]])
        for h in range(2):
            nc.vector.tensor_tensor(
                out=frac[:, halves[h]], in0=turns_flat[:, halves[h]], in1=whole_i[:, halves[h]], op=ALU.subtract
            )
        absn = const.tile([P, 512], F32, name="absn")
        trig = const.tile([P, 2, 2, 512], F32, name="trig")

        def build_trig(h):
            cols = halves[h]
            two_pi = 2.0 * PI
            nc.scalar.activation(out=trig[:, 1, 1, cols], in_=frac[:, cols], func=ACT.Sin, scale=two_pi)
            nc.scalar.activation(out=absn[:, cols], in_=frac[:, cols], func=ACT.Abs)
            nc.scalar.activation(out=trig[:, 0, 1, cols], in_=absn[:, cols], func=ACT.Sin, scale=-two_pi, bias=0.5 * PI)
            nc.scalar.activation(out=trig[:, 0, 0, cols], in_=frac[:, cols], func=ACT.Sin, scale=-two_pi)
            nc.scalar.activation(out=trig[:, 1, 0, cols], in_=absn[:, cols], func=ACT.Sin, scale=-two_pi, bias=0.5 * PI)

        grouped_e = const.tile([P, 8, 2, P, 4], BF16, name="grouped_e", align_bytes=64)
        grouped_e_flat = grouped_e[:].rearrange("p m g r j -> p (m g r j)")
        codes_e = const.tile([P, 2048], U32, name="codes_e", align_bytes=64)
        scales_e = const.tile([P, 2048], U8, name="scales_e", align_bytes=64)
        codes_w = {}
        scales_w = {}
        grouped_w = {}

        def transpose_block(words, warm=0):
            bank = psum.tile([P, 2, 2, P], F32, name="tp", tag="bank")
            for g in range(2):
                for u in range(2):
                    nc.tensor.transpose(bank[:, g, u, :], words[:, 256 * g + u : 256 * (g + 1) : 2], ident[:])
            return bank

        def copy_out(engine, dst, src):
            if engine == "S":
                nc.scalar.copy(out=dst, in_=src)
            else:
                nc.vector.tensor_copy(out=dst, in_=src)

        def evacuate(bank, dst, engines):
            if len(engines) == 1:
                copy_out(engines, dst, bank[:].rearrange("p g u r -> p g r u"))
            else:
                for g in range(2):
                    copy_out(engines[g], dst[:, g, :, :], bank[:, g, :, :].rearrange("p u r -> p r u"))

        def prep_emb(m, engines, warm=0):
            evacuate(transpose_block(emb_words[m], warm), grouped_e[:, m, :, :, :].bitcast(F32), engines)

        def quant_emb(first, count):
            lo = first * 256
            hi = (first + count) * 256
            nc.vector.quantize_mx(
                out=codes_e[:, lo:hi].bitcast(E5X4), scales=scales_e[:, lo:hi], in_=grouped_e_flat[:, 4 * lo : 4 * hi]
            )

        def open_weight(w, h):
            grouped_w[(w, h)] = grp.tile([P, 2, 512, 4], BF16, name="grouped_w", tag="grouped_w", align_bytes=64)
            codes_w[(w, h)] = const.tile([P, 1024], U32, name="codes_%s%d" % (w, h), align_bytes=64)
            scales_w[(w, h)] = const.tile([P, 1024], U8, name="scales_%s%d" % (w, h), align_bytes=64)

        def prep_block(w, h, i, engines, warm=0):
            gi, e = block_order(w)[i]
            evacuate(
                transpose_block(w_raw[(w, h)][:, gi, e, :].bitcast(F32), warm),
                grouped_w[(w, h)][:].bitcast(F32)[:, :, i * P : (i + 1) * P, :],
                engines,
            )

        def quant_weight(w, h, lo, hi):
            flat = grouped_w[(w, h)][:].rearrange("p g n j -> p (g n j)")
            nc.vector.quantize_mx(
                out=codes_w[(w, h)][:, lo:hi].bitcast(E5X4),
                scales=scales_w[(w, h)][:, lo:hi],
                in_=flat[:, 4 * lo : 4 * hi],
            )

        def project(w, m, h):
            acc = psum.tile([P, 512], F32, name="acc", tag="bank")
            for g in range(2):
                lo = (2 * m + g) * P
                nc.tensor.matmul_mx(
                    out=acc[:],
                    lhsT=codes_e[:, lo : lo + P].bitcast(E5X4),
                    lhsT_scale=scales_e[:, lo : lo + P],
                    rhs=codes_w[(w, h)][:, g * 512 : (g + 1) * 512].bitcast(E5X4),
                    rhs_scale=scales_w[(w, h)][:, g * 512 : (g + 1) * 512],
                    start=(g == 0),
                    stop=(g == 1),
                )
            return acc

        def rope_products(acc, h, prod, slot):
            nc.vector.tensor_tensor(
                out=prod[:, slot, :, :].rearrange("p s (x r) -> p s x r", r=2),
                in0=acc[:].rearrange("p (s x) -> p s x", s=2).unsqueeze(3).to_broadcast([P, 2, 256, 2]),
                in1=trig[:, :, :, h * 256 : (h + 1) * 256].rearrange("p s r x -> p s x r"),
                op=ALU.mult,
            )

        def store_pair(y, pair):
            (w, m0, h0), (w1, m1, h1) = pair
            if m0 == m1:
                nc.sync.dma_start(out=outs[w][m0 * P : (m0 + 1) * P, :], in_=y[:].rearrange("p b c -> p (b c)"))
            else:
                nc.sync.dma_start(
                    out=outs[w][m0 * P : (m0 + 2) * P, h0 * 512 : (h0 + 1) * 512].rearrange("(b p) c -> p b c", b=2),
                    in_=y[:],
                )

        def rope_sum_store(prod, pair, gcols):
            y = ypool.tile([P, 2, 512], F32, name="y", tag="y")
            if gcols < 512:
                vfirst = gcols - 8
                nc.vector.tensor_tensor(
                    out=y[:, :, vfirst:512], in0=prod[:, :, 0, vfirst:512], in1=prod[:, :, 1, vfirst:512], op=ALU.add
                )
            nc.gpsimd.tensor_tensor(
                out=y[:, :, 0:gcols], in0=prod[:, :, 0, 0:gcols], in1=prod[:, :, 1, 0:gcols], op=ALU.add
            )
            store_pair(y, pair)

        def quant_block(w, h, i):
            for g in range(2):
                quant_weight(w, h, g * 512 + i * P, g * 512 + (i + 1) * P)

        build_trig(0)
        prep_emb(0, "V", 0)
        open_weight("Q", 0)
        prep_block("Q", 0, 0, "V", 0)
        quant_emb(0, 1)
        quant_block("Q", 0, 0)
        prep_block("Q", 0, 1, "S", 0)
        prep_block("Q", 0, 2, "S", 0)
        quant_block("Q", 0, 1)
        prep_block("Q", 0, 3, "VS", 0)
        for g in range(2):
            for i in range(2, 4):
                quant_weight("Q", 0, g * 512 + i * P, g * 512 + (i + 1) * P)
        prep_emb(1, "S", 0)
        prep_emb(2, "S", 0)
        quant_emb(1, 1)

        pairs = [(("Q", m, h), ("Q", m + 1, h)) for h in range(2) for m in range(0, 8, 2)]
        pairs.extend([(("K", m, 0), ("K", m, 1)) for m in range(8)])
        chunks = [("Q", 1), ("V", 0), ("V", 1), ("K", 0), ("K", 1)]

        first = project("Q", 0, 0)
        prep_emb(3, "S")
        prep_emb(4, "S")
        accs = [first, project("Q", 1, 0)]
        waiting = {}

        def sum_waiting():
            prod_w, pair_w, j_w = waiting[0]
            rope_sum_store(prod_w, pair_w, GCOLS_BY_STEP.get(j_w, GCOLS))

        for j in range(16):
            pair = pairs[j]
            prod = tpool.tile([P, 2, 2, 512], F32, name="prod", tag="prod")
            rope_products(accs[0], pair[0][2], prod, 0)
            if j == 0:
                quant_emb(2, 1)
                quant_emb(3, 1)
            elif j == 1:
                quant_emb(4, 1)
                sum_waiting()
                quant_emb(5, 1)
            elif j == 2:
                quant_emb(6, 2)
                sum_waiting()
            else:
                if j - 3 < 5:
                    quant_weight(chunks[j - 3][0], chunks[j - 3][1], 0, 1024)
                sum_waiting()
            second = accs[1]
            if j < 15:
                accs = [project(w, m, h) for (w, m, h) in pairs[j + 1]]
            vaccs = []
            if j == 0:
                for m in range(5, 8):
                    prep_emb(m, "S")
                build_trig(1)
            elif j <= 5:
                open_weight(chunks[j - 1][0], chunks[j - 1][1])
                for i in range(4):
                    prep_block(chunks[j - 1][0], chunks[j - 1][1], i, "S")
            elif j < 14:
                vaccs = [project("V", j - 6, h) for h in range(2)]
            rope_products(second, pair[1][2], prod, 1)
            waiting[0] = (prod, pair, j)
            if vaccs:
                yv = vpool.tile([P, 2, 512], F32, name="yv", tag="yv")
                for h in range(2):
                    nc.scalar.copy(
                        out=yv[:, h, :].rearrange("p (x e) -> p x e", e=2),
                        in_=vaccs[h][:].rearrange("p (e x) -> p x e", e=2),
                    )
                mv = j - 6
                nc.scalar.dma_start(out=outs["V"][mv * P : (mv + 1) * P, :], in_=yv[:].rearrange("p b c -> p (b c)"))

        prod, pair, j = waiting[0]
        y = ypool.tile([P, 2, 512], F32, name="y", tag="y")
        for slot, lo, hi in ((0, 0, 512), (1, 0, 256), (1, 256, 512)):
            (w, m, h) = pair[slot]
            nc.vector.tensor_tensor(
                out=y[:, slot, lo:hi], in0=prod[:, slot, 0, lo:hi], in1=prod[:, slot, 1, lo:hi], op=ALU.add
            )
            nc.sync.dma_start(out=outs[w][m * P : (m + 1) * P, h * 512 + lo : h * 512 + hi], in_=y[:, slot, lo:hi])
